import numpy as np
import ml_dtypes


def mxq(x, axis, fmt="e4m3"):
    dtype, down = {"e4m3": (ml_dtypes.float8_e4m3fn, 7), "e5m2": (ml_dtypes.float8_e5m2, 14)}[fmt]
    v = np.moveaxis(np.asarray(x, np.float32).astype(ml_dtypes.bfloat16).astype(np.float64), axis, -1)
    blocks = v.reshape(v.shape[:-1] + (-1, 32))
    amax = np.abs(blocks).max(-1, keepdims=True)
    byte = np.maximum(np.where(amax > 0, np.frexp(amax)[1] - 1 + 127, 0) - down, 1)
    scale = np.exp2(byte - 127.0)
    codes = (blocks / scale).astype(np.float32).astype(dtype).astype(np.float64)
    return np.moveaxis((codes * scale).reshape(v.shape), -1, axis)


WIDE = False


def mx_kscale(k):
    if not WIDE:
        return np.ones(k)
    levels = np.array([10, -10, 5, -5, 0])
    a = np.random.permutation(np.resize(levels, k // 512 * 4)).reshape(k // 512, 4)
    idx = np.arange(k)
    return np.exp2(a[idx // 512, idx % 128 // 32])


BF16 = ml_dtypes.bfloat16


def bf(x):
    return np.asarray(x, np.float32).astype(BF16)


def f64(x):
    return np.asarray(x).astype(np.float64)


B, S, D, E = 2, 512, 512, 512
SC = 1.5


def setup_inputs():
    s, t = mx_kscale(D), mx_kscale(E)
    rn = np.random.standard_normal
    qs = np.sqrt(SC / np.sqrt(2.0 * E))
    ws = qs / np.sqrt(2.0 * D)
    return {"x_re": bf(rn((B, S, D)) * s), "x_im": bf(rn((B, S, D)) * s),
            "Wq_re": bf(rn((E, D)) * ws * t[:, None] / s), "Wq_im": bf(rn((E, D)) * ws * t[:, None] / s),
            "bq_re": bf(rn(E) * 0.5 * qs * t), "bq_im": bf(rn(E) * 0.5 * qs * t),
            "Wk_re": bf(rn((E, D)) * ws / t[:, None] / s), "Wk_im": bf(rn((E, D)) * ws / t[:, None] / s),
            "bk_re": bf(rn(E) * 0.5 * qs / t), "bk_im": bf(rn(E) * 0.5 * qs / t)}


def cproj(xr, xi, w_re, w_im, b_re, b_im):
    wr = mxq(f64(w_re), 1, "e4m3").T
    wi = mxq(f64(w_im), 1, "e4m3").T
    y_re = (xr @ wr) - (xi @ wi) + f64(b_re)
    y_im = (xr @ wi) + (xi @ wr) + f64(b_im)
    return y_re, y_im


def reference(x_re, x_im, Wq_re, Wq_im, bq_re, bq_im, Wk_re, Wk_im, bk_re, bk_im):
    xr = mxq(f64(x_re), 2, "e4m3")
    xi = mxq(f64(x_im), 2, "e4m3")
    q_re, q_im = cproj(xr, xi, Wq_re, Wq_im, bq_re, bq_im)
    k_re, k_im = cproj(xr, xi, Wk_re, Wk_im, bk_re, bk_im)
    return ((mxq(q_re, 2, "e4m3") @ mxq(k_re, 2, "e4m3").transpose(0, 2, 1))
            + (mxq(q_im, 2, "e4m3") @ mxq(k_im, 2, "e4m3").transpose(0, 2, 1)))

@@ -1,0 +1,207 @@
+from contextlib import ExitStack
+
+import concourse.mybir as mybir
+from concourse.masks import make_identity
+
+F32 = mybir.dt.float32
+BF16 = mybir.dt.bfloat16
+U32 = mybir.dt.uint32
+U8 = mybir.dt.uint8
+FP8X4 = mybir.dt.float8_e4m3fn_x4
+
+P = 128
+PACK = 4
+BANK = 512
+BATCH = 2
+TOKENS = 512
+FEATURES = 512
+GROUPS = 4
+BLOCKS = 2 * GROUPS
+ROUND = 2
+SCORE_LAG = 3
+RE = 0
+IM = 1
+
+FLOPS = 8 * 2 * BATCH * TOKENS * FEATURES * FEATURES + 2 * 2 * BATCH * TOKENS * TOKENS * FEATURES
+
+
+def new_mx_operand(pool, name, columns):
+    codes = pool.tile([P, columns], U32, name=name + "_codes", align_bytes=64)
+    scales = pool.tile([P, columns], U8, name=name + "_scales", align_bytes=64)
+    return {"codes": codes, "scales": scales}
+
+
+def quantise(nc, operand, first, values):
+    columns = slice(first, first + values.shape[1] // PACK)
+    nc.vector.quantize_mx(
+        out=operand["codes"][:, columns].bitcast(FP8X4),
+        scales=operand["scales"][:, columns],
+        in_=values,
+    )
+
+
+def mx_pass(nc, acc, stationary, s_first, moving, m_first, start, stop):
+    s_columns = slice(s_first, s_first + P)
+    m_columns = slice(m_first, m_first + acc.shape[1])
+    nc.tensor.matmul_mx(
+        out=acc,
+        lhsT=stationary["codes"][:, s_columns].bitcast(FP8X4),
+        lhsT_scale=stationary["scales"][:, s_columns],
+        rhs=moving["codes"][:, m_columns].bitcast(FP8X4),
+        rhs_scale=moving["scales"][:, m_columns],
+        start=start,
+        stop=stop,
+    )
+
+
+def tile_teleportationattention_pa_kernel(
+    tc, x_re, x_im, Wq_re, Wq_im, bq_re, bq_im, Wk_re, Wk_im, bk_re, bk_im, out
+):
+    nc = tc.nc
+    with ExitStack() as ctx:
+        keep = ctx.enter_context(tc.tile_pool(name="keep", bufs=1))
+        work = ctx.enter_context(tc.tile_pool(name="work", bufs=3))
+        psum = ctx.enter_context(tc.psum_pool(name="psum", bufs=8))
+
+        ident = keep.tile([P, P], F32, name="ident")
+        make_identity(nc, ident[:])
+
+        bias_slots = keep.tile([P, 4, 16], BF16, name="bias_slots")
+        bias = {}
+        for n, (kind, part, vector) in enumerate(
+            (("k", RE, bk_re), ("k", IM, bk_im), ("q", RE, bq_re), ("q", IM, bq_im))
+        ):
+            bias[kind, part] = bias_slots[:, n, 0:PACK]
+            nc.gpsimd.dma_start(out=bias[kind, part], in_=vector.rearrange("(r t) -> r t", t=PACK))
+
+        def load(name, matrix):
+            raw = keep.tile([P, GROUPS * FEATURES], BF16, name=name)
+            nc.sync.dma_start(out=raw[:], in_=matrix.rearrange("(r j) d -> r (j d)", j=GROUPS))
+            return raw
+
+        raw_w = {}
+        raw_x = {}
+        raw_w["k", RE] = load("raw_wk_re", Wk_re)
+        raw_w["k", IM] = load("raw_wk_im", Wk_im)
+        raw_x[0, RE] = load("raw_x0_re", x_re[0, :, :])
+        raw_x[0, IM] = load("raw_x0_im", x_im[0, :, :])
+        raw_w["q", RE] = load("raw_wq_re", Wq_re)
+        raw_w["q", IM] = load("raw_wq_im", Wq_im)
+        raw_x[1, RE] = load("raw_x1_re", x_re[1, :, :])
+        raw_x[1, IM] = load("raw_x1_im", x_im[1, :, :])
+
+        weight = {}
+        for kind in ("k", "q"):
+            for part in ("re", "im", "im_neg"):
+                weight[kind, part] = new_mx_operand(keep, "w" + kind + "_" + part, FEATURES)
+        tokens = {
+            RE: new_mx_operand(keep, "x_re", BATCH * TOKENS),
+            IM: new_mx_operand(keep, "x_im", BATCH * TOKENS),
+        }
+        projected = {kind: new_mx_operand(keep, kind, BATCH * BLOCKS * P) for kind in ("k", "q")}
+
+        block_order = {
+            "k": [(part, j) for part in (RE, IM) for j in range(GROUPS)],
+            "q": [(part, j) for j in range(GROUPS) for part in (RE, IM)],
+        }
+
+        def first_column(kind, b, part, j):
+            return (b * BLOCKS + block_order[kind].index((part, j))) * P
+
+        def features_to_partitions(raw):
+            raw_words = raw[:].bitcast(F32)
+            grouped = work.tile([P, GROUPS * P * PACK], BF16, tag="grouped_in", align_bytes=64)
+            grouped_words = grouped[:].bitcast(F32)
+            for half in range(2):
+                bank = psum.tile([P, BANK], F32, tag="bank")
+                for s in range(4):
+                    nc.tensor.transpose(
+                        bank[:, s * P : (s + 1) * P],
+                        raw_words[:, half * BANK + s * P : half * BANK + (s + 1) * P],
+                        ident[:],
+                    )
+                nc.scalar.copy(
+                    out=grouped_words[:, half * BANK : (half + 1) * BANK].rearrange(
+                        "p (j r u) -> p j r u", j=2, u=2
+                    ),
+                    in_=bank[:].rearrange("p (j u r) -> p j r u", j=2, u=2),
+                )
+            return grouped
+
+        def prepare_weights(kind):
+            quantise(nc, weight[kind, "re"], 0, features_to_partitions(raw_w[kind, RE])[:])
+            grouped = features_to_partitions(raw_w[kind, IM])
+            negated = work.tile([P, GROUPS * P * PACK], BF16, tag="negated", align_bytes=64)
+            nc.vector.tensor_scalar_mul(out=negated[:], in0=grouped[:], scalar1=-1.0)
+            quantise(nc, weight[kind, "im"], 0, grouped[:])
+            quantise(nc, weight[kind, "im_neg"], 0, negated[:])
+
+        def prepare_tokens(b):
+            for part in (RE, IM):
+                quantise(nc, tokens[part], b * TOKENS, features_to_partitions(raw_x[b, part])[:])
+
+        def project_round(kind, b, first_block):
+            grouped = work.tile([P, ROUND * BANK], BF16, tag="grouped_y", align_bytes=64)
+            for s in range(ROUND):
+                part, j = block_order[kind][first_block + s]
+                w_of_x_re, w_of_x_im = (("re", "im_neg"), ("im", "re"))[part]
+                bank = psum.tile([P, BANK], F32, tag="bank")
+                for t in range(PACK):
+                    acc = bank[:, t * P : (t + 1) * P]
+                    x_first = b * TOKENS + j * P
+                    mx_pass(nc, acc, weight[kind, w_of_x_re], t * P, tokens[RE], x_first, True, False)
+                    mx_pass(nc, acc, weight[kind, w_of_x_im], t * P, tokens[IM], x_first, False, True)
+                nc.vector.tensor_tensor(
+                    out=grouped[:, s * BANK : (s + 1) * BANK].rearrange("p (r t) -> p r t", t=PACK),
+                    in0=bank[:].rearrange("p (t r) -> p r t", t=PACK),
+                    in1=bias[kind, part].unsqueeze(1).to_broadcast([P, P, PACK]),
+                    op=mybir.AluOpType.add,
+                )
+            return grouped
+
+        def score_rows(b, j):
+            acc = psum.tile([P, BANK], F32, tag="bank")
+            for part in (RE, IM):
+                mx_pass(
+                    nc,
+                    acc[:],
+                    projected["q"],
+                    first_column("q", b, part, j),
+                    projected["k"],
+                    first_column("k", b, part, 0),
+                    part == RE,
+                    part == IM,
+                )
+            rows = work.tile([P, TOKENS], F32, tag="rows")
+            nc.scalar.copy(
+                out=rows[:].rearrange("p (r g) -> p r g", g=GROUPS),
+                in_=acc[:].rearrange("p (g r) -> p r g", g=GROUPS),
+            )
+            nc.sync.dma_start(
+                out=out[b, :, :].rearrange("(r j) k -> r j k", j=GROUPS)[:, j, :], in_=rows[:]
+            )
+
+        prepare_weights("k")
+        prepare_tokens(0)
+        prepare_weights("q")
+
+        rounds = [
+            (kind, b, first_block)
+            for b in range(BATCH)
+            for kind in ("k", "q")
+            for first_block in range(0, BLOCKS, ROUND)
+        ]
+        values = {}
+        for step in range(len(rounds) + SCORE_LAG):
+            if step < len(rounds):
+                kind, b, first_block = rounds[step]
+                if kind == "q" and first_block == 0 and b + 1 < BATCH:
+                    prepare_tokens(b + 1)
+                values[step] = project_round(kind, b, first_block)
+            if 1 <= step <= len(rounds):
+                kind, b, first_block = rounds[step - 1]
+                quantise(nc, projected[kind], (b * BLOCKS + first_block) * P, values[step - 1][:])
+            if step >= SCORE_LAG:
+                kind, b, first_block = rounds[step - SCORE_LAG]
+                if kind == "q":
+                    score_rows(b, block_order["q"][first_block][1])

@@ -19,6 +19,7 @@ GROUPS = 4
 BLOCKS = 2 * GROUPS
 ROUND = 2
 SCORE_LAG = 3
+SCALAR_EVERY = 3
 RE = 0
 IM = 1
 
@@ -67,12 +68,16 @@ def tile_teleportationattention_pa_kernel(
         make_identity(nc, ident[:])
 
         bias_slots = keep.tile([P, 4, 16], BF16, name="bias_slots")
+        bias_f32 = keep.tile([P, 4, PACK], F32, name="bias_f32")
         bias = {}
         for n, (kind, part, vector) in enumerate(
             (("k", RE, bk_re), ("k", IM, bk_im), ("q", RE, bq_re), ("q", IM, bq_im))
         ):
-            bias[kind, part] = bias_slots[:, n, 0:PACK]
-            nc.gpsimd.dma_start(out=bias[kind, part], in_=vector.rearrange("(r t) -> r t", t=PACK))
+            nc.gpsimd.dma_start(
+                out=bias_slots[:, n, 0:PACK], in_=vector.rearrange("(r t) -> r t", t=PACK)
+            )
+            bias[kind, part] = bias_f32[:, n, :]
+            nc.vector.tensor_copy(out=bias[kind, part], in_=bias_slots[:, n, 0:PACK])
 
         def load(name, matrix):
             raw = keep.tile([P, GROUPS * FEATURES], BF16, name=name)
@@ -140,7 +145,7 @@ def tile_teleportationattention_pa_kernel(
             for part in (RE, IM):
                 quantise(nc, tokens[part], b * TOKENS, features_to_partitions(raw_x[b, part])[:])
 
-        def project_round(kind, b, first_block):
+        def project_round(kind, b, first_block, scalar_helps):
             grouped = work.tile([P, ROUND * BANK], BF16, tag="grouped_y", align_bytes=64)
             for s in range(ROUND):
                 part, j = block_order[kind][first_block + s]
@@ -151,12 +156,23 @@ def tile_teleportationattention_pa_kernel(
                     x_first = b * TOKENS + j * P
                     mx_pass(nc, acc, weight[kind, w_of_x_re], t * P, tokens[RE], x_first, True, False)
                     mx_pass(nc, acc, weight[kind, w_of_x_im], t * P, tokens[IM], x_first, False, True)
-                nc.vector.tensor_tensor(
-                    out=grouped[:, s * BANK : (s + 1) * BANK].rearrange("p (r t) -> p r t", t=PACK),
-                    in0=bank[:].rearrange("p (t r) -> p r t", t=PACK),
-                    in1=bias[kind, part].unsqueeze(1).to_broadcast([P, P, PACK]),
-                    op=mybir.AluOpType.add,
-                )
+                quads = grouped[:, s * BANK : (s + 1) * BANK].rearrange("p (r t) -> p r t", t=PACK)
+                if scalar_helps and s == 0:
+                    for t in range(PACK):
+                        nc.scalar.activation(
+                            out=quads[:, :, t],
+                            in_=bank[:, t * P : (t + 1) * P],
+                            func=mybir.ActivationFunctionType.Identity,
+                            bias=bias[kind, part][:, t : t + 1],
+                            scale=1.0,
+                        )
+                else:
+                    nc.vector.tensor_tensor(
+                        out=quads,
+                        in0=bank[:].rearrange("p (t r) -> p r t", t=PACK),
+                        in1=bias[kind, part].unsqueeze(1).to_broadcast([P, P, PACK]),
+                        op=mybir.AluOpType.add,
+                    )
             return grouped
 
         def score_rows(b, j):
@@ -197,7 +213,7 @@ def tile_teleportationattention_pa_kernel(
                 kind, b, first_block = rounds[step]
                 if kind == "q" and first_block == 0 and b + 1 < BATCH:
                     prepare_tokens(b + 1)
-                values[step] = project_round(kind, b, first_block)
+                values[step] = project_round(kind, b, first_block, step % SCALAR_EVERY == 1)
             if 1 <= step <= len(rounds):
                 kind, b, first_block = rounds[step - 1]
                 quantise(nc, projected[kind], (b * BLOCKS + first_block) * P, values[step - 1][:])

@@ -16,10 +16,8 @@ BATCH = 2
 TOKENS = 512
 FEATURES = 512
 GROUPS = 4
-BLOCKS = 2 * GROUPS
-ROUND = 2
+PIECE = 2 * FEATURES
 SCORE_LAG = 3
-SCALAR_EVERY = 3
 RE = 0
 IM = 1
 
@@ -61,119 +59,143 @@ def tile_teleportationattention_pa_kernel(
     nc = tc.nc
     with ExitStack() as ctx:
         keep = ctx.enter_context(tc.tile_pool(name="keep", bufs=1))
-        work = ctx.enter_context(tc.tile_pool(name="work", bufs=3))
+        work = ctx.enter_context(tc.tile_pool(name="work", bufs=4))
         psum = ctx.enter_context(tc.psum_pool(name="psum", bufs=8))
+        ctx.enter_context(tc.manual_schedule())
 
         ident = keep.tile([P, P], F32, name="ident")
         make_identity(nc, ident[:])
 
         bias_slots = keep.tile([P, 4, 16], BF16, name="bias_slots")
-        bias_f32 = keep.tile([P, 4, PACK], F32, name="bias_f32")
         bias = {}
         for n, (kind, part, vector) in enumerate(
-            (("k", RE, bk_re), ("k", IM, bk_im), ("q", RE, bq_re), ("q", IM, bq_im))
+            (("q", RE, bq_re), ("q", IM, bq_im), ("k", RE, bk_re), ("k", IM, bk_im))
         ):
-            nc.gpsimd.dma_start(
-                out=bias_slots[:, n, 0:PACK], in_=vector.rearrange("(r t) -> r t", t=PACK)
-            )
-            bias[kind, part] = bias_f32[:, n, :]
-            nc.vector.tensor_copy(out=bias[kind, part], in_=bias_slots[:, n, 0:PACK])
+            bias[kind, part] = bias_slots[:, n, 0:PACK]
+            nc.scalar.dma_start(out=bias[kind, part], in_=vector.rearrange("(r t) -> r t", t=PACK))
 
-        def load(name, matrix):
-            raw = keep.tile([P, GROUPS * FEATURES], BF16, name=name)
-            nc.sync.dma_start(out=raw[:], in_=matrix.rearrange("(r j) d -> r (j d)", j=GROUPS))
+        def load(name, matrix, first_group, groups):
+            raw = keep.tile([P, groups * FEATURES], BF16, name=name)
+            by_partition = matrix.rearrange("(r j) d -> r (j d)", j=GROUPS)
+            first = first_group * FEATURES
+            nc.sync.dma_start(out=raw[:], in_=by_partition[:, first : first + groups * FEATURES])
             return raw
 
         raw_w = {}
         raw_x = {}
-        raw_w["k", RE] = load("raw_wk_re", Wk_re)
-        raw_w["k", IM] = load("raw_wk_im", Wk_im)
-        raw_x[0, RE] = load("raw_x0_re", x_re[0, :, :])
-        raw_x[0, IM] = load("raw_x0_im", x_im[0, :, :])
-        raw_w["q", RE] = load("raw_wq_re", Wq_re)
-        raw_w["q", IM] = load("raw_wq_im", Wq_im)
-        raw_x[1, RE] = load("raw_x1_re", x_re[1, :, :])
-        raw_x[1, IM] = load("raw_x1_im", x_im[1, :, :])
+
+        def load_weights(kind, w_re, w_im):
+            for part, name, matrix in ((IM, "im", w_im), (RE, "re", w_re)):
+                whole = load("raw_w" + kind + "_" + name, matrix, 0, GROUPS)
+                raw_w[kind, part] = [whole[:, 0:PIECE], whole[:, PIECE : 2 * PIECE]]
+
+        def load_tokens(b):
+            raw_x[b, RE] = []
+            raw_x[b, IM] = []
+            for half in range(2):
+                tail = str(b) + "_" + str(half)
+                raw_x[b, RE].append(load("raw_x_re" + tail, x_re[b, :, :], 2 * half, 2)[:])
+                raw_x[b, IM].append(load("raw_x_im" + tail, x_im[b, :, :], 2 * half, 2)[:])
+
+        load_weights("q", Wq_re, Wq_im)
+        load_tokens(0)
+        load_weights("k", Wk_re, Wk_im)
+        load_tokens(1)
 
         weight = {}
         for kind in ("k", "q"):
-            for part in ("re", "im", "im_neg"):
-                weight[kind, part] = new_mx_operand(keep, "w" + kind + "_" + part, FEATURES)
-        tokens = {
-            RE: new_mx_operand(keep, "x_re", BATCH * TOKENS),
-            IM: new_mx_operand(keep, "x_im", BATCH * TOKENS),
-        }
-        projected = {kind: new_mx_operand(keep, kind, BATCH * BLOCKS * P) for kind in ("k", "q")}
+            for name in ("re", "im", "im_neg"):
+                weight[kind, name] = new_mx_operand(keep, "w" + kind + "_" + name, FEATURES)
+        tokens = new_mx_operand(keep, "x", BATCH * 2 * TOKENS)
+        keys = new_mx_operand(keep, "k", BATCH * 2 * TOKENS)
+        queries = new_mx_operand(keep, "q", BATCH * 2 * TOKENS)
 
-        block_order = {
-            "k": [(part, j) for part in (RE, IM) for j in range(GROUPS)],
-            "q": [(part, j) for j in range(GROUPS) for part in (RE, IM)],
-        }
+        def part_major_column(b, part, j):
+            return ((b * 2 + part) * GROUPS + j) * P
 
-        def first_column(kind, b, part, j):
-            return (b * BLOCKS + block_order[kind].index((part, j))) * P
+        def group_major_column(b, part, j):
+            return ((b * GROUPS + j) * 2 + part) * P
 
-        def features_to_partitions(raw):
-            raw_words = raw[:].bitcast(F32)
-            grouped = work.tile([P, GROUPS * P * PACK], BF16, tag="grouped_in", align_bytes=64)
-            grouped_words = grouped[:].bitcast(F32)
+        def features_to_partitions(piece):
+            raw_pairs = piece.bitcast(F32)
+            grouped = work.tile([P, PIECE], BF16, tag="grouped_in", bufs=8, align_bytes=64)
+            bank = psum.tile([P, BANK], F32, tag="bank")
+            for s in range(4):
+                columns = slice(s * P, (s + 1) * P)
+                nc.tensor.transpose(bank[:, columns], raw_pairs[:, columns], ident[:])
+            nc.scalar.copy(
+                out=grouped[:].bitcast(F32).rearrange("p (j r u) -> p j r u", j=2, u=2),
+                in_=bank[:].rearrange("p (j u r) -> p j r u", j=2, u=2),
+            )
+            return grouped
+
+        def transpose_weights(kind):
+            return {part: [features_to_partitions(piece) for piece in raw_w[kind, part]] for part in (IM, RE)}
+
+        def quantise_weights(kind, grouped):
             for half in range(2):
+                first = half * PIECE // PACK
+                negated = work.tile([P, PIECE], BF16, tag="negated", align_bytes=64)
+                nc.vector.tensor_scalar_mul(out=negated[:], in0=grouped[IM][half][:], scalar1=-1.0)
+                quantise(nc, weight[kind, "im"], first, grouped[IM][half][:])
+                quantise(nc, weight[kind, "im_neg"], first, negated[:])
+            for half in range(2):
+                quantise(nc, weight[kind, "re"], half * PIECE // PACK, grouped[RE][half][:])
+
+        def transpose_tokens(b):
+            return [{part: features_to_partitions(raw_x[b, part][half]) for part in (RE, IM)} for half in range(2)]
+
+        def quantise_tokens(b, grouped):
+            for half in range(2):
+                for part in (RE, IM):
+                    quantise(nc, tokens, part_major_column(b, part, 2 * half), grouped[half][part][:])
+
+        def project(acc, kind, part, t, b, j):
+            w_of_x_re, w_of_x_im = (("re", "im_neg"), ("im", "re"))[part]
+            mx_pass(nc, acc, weight[kind, w_of_x_re], t * P, tokens, part_major_column(b, RE, j), True, False)
+            mx_pass(nc, acc, weight[kind, w_of_x_im], t * P, tokens, part_major_column(b, IM, j), False, True)
+
+        def project_queries(b, j):
+            grouped = work.tile([P, 2 * BANK], BF16, tag="grouped_q", align_bytes=64)
+            for part in (RE, IM):
                 bank = psum.tile([P, BANK], F32, tag="bank")
-                for s in range(4):
-                    nc.tensor.transpose(
-                        bank[:, s * P : (s + 1) * P],
-                        raw_words[:, half * BANK + s * P : half * BANK + (s + 1) * P],
-                        ident[:],
-                    )
-                nc.scalar.copy(
-                    out=grouped_words[:, half * BANK : (half + 1) * BANK].rearrange(
-                        "p (j r u) -> p j r u", j=2, u=2
-                    ),
-                    in_=bank[:].rearrange("p (j u r) -> p j r u", j=2, u=2),
+                for t in range(PACK):
+                    project(bank[:, t * P : (t + 1) * P], "q", part, t, b, j)
+                nc.vector.tensor_tensor(
+                    out=grouped[:, part * BANK : (part + 1) * BANK].rearrange("p (n t) -> p n t", t=PACK),
+                    in0=bank[:].rearrange("p (t n) -> p n t", t=PACK),
+                    in1=bias["q", part].unsqueeze(1).to_broadcast([P, P, PACK]),
+                    op=mybir.AluOpType.add,
                 )
             return grouped
 
-        def prepare_weights(kind):
-            quantise(nc, weight[kind, "re"], 0, features_to_partitions(raw_w[kind, RE])[:])
-            grouped = features_to_partitions(raw_w[kind, IM])
-            negated = work.tile([P, GROUPS * P * PACK], BF16, tag="negated", align_bytes=64)
-            nc.vector.tensor_scalar_mul(out=negated[:], in0=grouped[:], scalar1=-1.0)
-            quantise(nc, weight[kind, "im"], 0, grouped[:])
-            quantise(nc, weight[kind, "im_neg"], 0, negated[:])
+        def quantise_queries(b, j, grouped):
+            quantise(nc, queries, group_major_column(b, RE, j), grouped[:])
 
-        def prepare_tokens(b):
-            for part in (RE, IM):
-                quantise(nc, tokens[part], b * TOKENS, features_to_partitions(raw_x[b, part])[:])
-
-        def project_round(kind, b, first_block, scalar_helps):
-            grouped = work.tile([P, ROUND * BANK], BF16, tag="grouped_y", align_bytes=64)
-            for s in range(ROUND):
-                part, j = block_order[kind][first_block + s]
-                w_of_x_re, w_of_x_im = (("re", "im_neg"), ("im", "re"))[part]
+        def project_keys(b, part):
+            planes = work.tile([P, PACK * TOKENS], BF16, tag="planes", bufs=2)
+            for t in range(PACK):
                 bank = psum.tile([P, BANK], F32, tag="bank")
-                for t in range(PACK):
-                    acc = bank[:, t * P : (t + 1) * P]
-                    x_first = b * TOKENS + j * P
-                    mx_pass(nc, acc, weight[kind, w_of_x_re], t * P, tokens[RE], x_first, True, False)
-                    mx_pass(nc, acc, weight[kind, w_of_x_im], t * P, tokens[IM], x_first, False, True)
-                quads = grouped[:, s * BANK : (s + 1) * BANK].rearrange("p (r t) -> p r t", t=PACK)
-                if scalar_helps and s == 0:
-                    for t in range(PACK):
-                        nc.scalar.activation(
-                            out=quads[:, :, t],
-                            in_=bank[:, t * P : (t + 1) * P],
-                            func=mybir.ActivationFunctionType.Identity,
-                            bias=bias[kind, part][:, t : t + 1],
-                            scale=1.0,
-                        )
-                else:
-                    nc.vector.tensor_tensor(
-                        out=quads,
-                        in0=bank[:].rearrange("p (t r) -> p r t", t=PACK),
-                        in1=bias[kind, part].unsqueeze(1).to_broadcast([P, P, PACK]),
-                        op=mybir.AluOpType.add,
-                    )
+                project(bank[:], "k", part, t, b, 0)
+                nc.scalar.activation(
+                    out=planes[:, t * TOKENS : (t + 1) * TOKENS],
+                    in_=bank[:],
+                    func=mybir.ActivationFunctionType.Identity,
+                    bias=bias["k", part][:, t : t + 1],
+                    scale=1.0,
+                )
+            return planes
+
+        def interleave_keys(planes):
+            grouped = work.tile([P, PACK * TOKENS], BF16, tag="grouped_k", bufs=2, align_bytes=64)
+            nc.vector.tensor_copy(
+                out=grouped[:].rearrange("p (c i t) -> p c t i", i=4, t=PACK),
+                in_=planes[:].rearrange("p (t c i) -> p c t i", i=4, t=PACK),
+            )
             return grouped
+
+        def quantise_keys(b, part, grouped):
+            quantise(nc, keys, part_major_column(b, part, 0), grouped[:])
 
         def score_rows(b, j):
             acc = psum.tile([P, BANK], F32, tag="bank")
@@ -181,10 +203,10 @@ def tile_teleportationattention_pa_kernel(
                 mx_pass(
                     nc,
                     acc[:],
-                    projected["q"],
-                    first_column("q", b, part, j),
-                    projected["k"],
-                    first_column("k", b, part, 0),
+                    queries,
+                    group_major_column(b, part, j),
+                    keys,
+                    part_major_column(b, part, 0),
                     part == RE,
                     part == IM,
                 )
@@ -197,27 +219,42 @@ def tile_teleportationattention_pa_kernel(
                 out=out[b, :, :].rearrange("(r j) k -> r j k", j=GROUPS)[:, j, :], in_=rows[:]
             )
 
-        prepare_weights("k")
-        prepare_tokens(0)
-        prepare_weights("q")
 
-        rounds = [
-            (kind, b, first_block)
-            for b in range(BATCH)
-            for kind in ("k", "q")
-            for first_block in range(0, BLOCKS, ROUND)
-        ]
-        values = {}
-        for step in range(len(rounds) + SCORE_LAG):
-            if step < len(rounds):
-                kind, b, first_block = rounds[step]
-                if kind == "q" and first_block == 0 and b + 1 < BATCH:
-                    prepare_tokens(b + 1)
-                values[step] = project_round(kind, b, first_block, step % SCALAR_EVERY == 1)
-            if 1 <= step <= len(rounds):
-                kind, b, first_block = rounds[step - 1]
-                quantise(nc, projected[kind], (b * BLOCKS + first_block) * P, values[step - 1][:])
-            if step >= SCORE_LAG:
-                kind, b, first_block = rounds[step - SCORE_LAG]
-                if kind == "q":
-                    score_rows(b, block_order["q"][first_block][1])
+        quantise_weights("q", transpose_weights("q"))
+        quantise_tokens(0, transpose_tokens(0))
+        q_values = {}
+        for j in range(GROUPS):
+            q_values[j] = project_queries(0, j)
+            if j == 0:
+                wk_grouped = transpose_weights("k")
+            if j == 1:
+                x1_grouped = transpose_tokens(1)
+            if j > 0:
+                quantise_queries(0, j - 1, q_values[j - 1])
+            if j == 1:
+                quantise_weights("k", wk_grouped)
+            if j == 2:
+                quantise_tokens(1, x1_grouped)
+        quantise_queries(0, GROUPS - 1, q_values[GROUPS - 1])
+
+        units = [(b, part) for b in range(BATCH) for part in (RE, IM)]
+        k_planes = {}
+        k_values = {}
+        for n in range(len(units) + 2):
+            if n < len(units):
+                k_planes[n] = project_keys(units[n][0], units[n][1])
+            if 1 <= n <= len(units):
+                k_values[n - 1] = interleave_keys(k_planes[n - 1])
+            if n >= 2:
+                quantise_keys(units[n - 2][0], units[n - 2][1], k_values[n - 2])
+                if units[n - 2] == (0, IM):
+                    for j in range(GROUPS):
+                        score_rows(0, j)
+
+        for j in range(GROUPS + SCORE_LAG):
+            if j < GROUPS:
+                q_values[j] = project_queries(1, j)
+            if 1 <= j <= GROUPS:
+                quantise_queries(1, j - 1, q_values[j - 1])
+            if j >= SCORE_LAG:
+                score_rows(1, j - SCORE_LAG)

from contextlib import ExitStack

import concourse.mybir as mybir
from concourse.masks import make_identity

F32 = mybir.dt.float32
BF16 = mybir.dt.bfloat16
U32 = mybir.dt.uint32
U8 = mybir.dt.uint8
FP8X4 = mybir.dt.float8_e4m3fn_x4

P = 128
PACK = 4
BANK = 512
BATCH = 2
TOKENS = 512
FEATURES = 512
GROUPS = 4
PIECE = 2 * FEATURES
SCORE_LAG = 3
RE = 0
IM = 1

FLOPS = 8 * 2 * BATCH * TOKENS * FEATURES * FEATURES + 2 * 2 * BATCH * TOKENS * TOKENS * FEATURES


def new_mx_operand(pool, name, columns):
    codes = pool.tile([P, columns], U32, name=name + "_codes", align_bytes=64)
    scales = pool.tile([P, columns], U8, name=name + "_scales", align_bytes=64)
    return {"codes": codes, "scales": scales}


def quantise(nc, operand, first, values):
    columns = slice(first, first + values.shape[1] // PACK)
    nc.vector.quantize_mx(
        out=operand["codes"][:, columns].bitcast(FP8X4),
        scales=operand["scales"][:, columns],
        in_=values,
    )


def mx_pass(nc, acc, stationary, s_first, moving, m_first, start, stop):
    s_columns = slice(s_first, s_first + P)
    m_columns = slice(m_first, m_first + acc.shape[1])
    nc.tensor.matmul_mx(
        out=acc,
        lhsT=stationary["codes"][:, s_columns].bitcast(FP8X4),
        lhsT_scale=stationary["scales"][:, s_columns],
        rhs=moving["codes"][:, m_columns].bitcast(FP8X4),
        rhs_scale=moving["scales"][:, m_columns],
        start=start,
        stop=stop,
    )


def tile_teleportationattention_pa_kernel(
    tc, x_re, x_im, Wq_re, Wq_im, bq_re, bq_im, Wk_re, Wk_im, bk_re, bk_im, out
):
    nc = tc.nc
    with ExitStack() as ctx:
        keep = ctx.enter_context(tc.tile_pool(name="keep", bufs=1))
        work = ctx.enter_context(tc.tile_pool(name="work", bufs=4))
        psum = ctx.enter_context(tc.psum_pool(name="psum", bufs=8))
        ctx.enter_context(tc.manual_schedule())

        ident = keep.tile([P, P], F32, name="ident")
        make_identity(nc, ident[:])

        bias_slots = keep.tile([P, 4, 16], BF16, name="bias_slots")
        bias = {}
        for n, (kind, part, vector) in enumerate(
            (("q", RE, bq_re), ("q", IM, bq_im), ("k", RE, bk_re), ("k", IM, bk_im))
        ):
            bias[kind, part] = bias_slots[:, n, 0:PACK]
            nc.scalar.dma_start(out=bias[kind, part], in_=vector.rearrange("(r t) -> r t", t=PACK))

        def load(name, matrix, first_group, groups):
            raw = keep.tile([P, groups * FEATURES], BF16, name=name)
            by_partition = matrix.rearrange("(r j) d -> r (j d)", j=GROUPS)
            first = first_group * FEATURES
            nc.sync.dma_start(out=raw[:], in_=by_partition[:, first : first + groups * FEATURES])
            return raw

        raw_w = {}
        raw_x = {}

        def load_weights(kind, w_re, w_im):
            for part, name, matrix in ((IM, "im", w_im), (RE, "re", w_re)):
                whole = load("raw_w" + kind + "_" + name, matrix, 0, GROUPS)
                raw_w[kind, part] = [whole[:, 0:PIECE], whole[:, PIECE : 2 * PIECE]]

        def load_tokens(b):
            raw_x[b, RE] = []
            raw_x[b, IM] = []
            for half in range(2):
                tail = str(b) + "_" + str(half)
                raw_x[b, RE].append(load("raw_x_re" + tail, x_re[b, :, :], 2 * half, 2)[:])
                raw_x[b, IM].append(load("raw_x_im" + tail, x_im[b, :, :], 2 * half, 2)[:])

        load_weights("q", Wq_re, Wq_im)
        load_tokens(0)
        load_weights("k", Wk_re, Wk_im)
        load_tokens(1)

        weight = {}
        for kind in ("k", "q"):
            for name in ("re", "im", "im_neg"):
                weight[kind, name] = new_mx_operand(keep, "w" + kind + "_" + name, FEATURES)
        tokens = new_mx_operand(keep, "x", BATCH * 2 * TOKENS)
        keys = new_mx_operand(keep, "k", BATCH * 2 * TOKENS)
        queries = new_mx_operand(keep, "q", BATCH * 2 * TOKENS)

        def part_major_column(b, part, j):
            return ((b * 2 + part) * GROUPS + j) * P

        def group_major_column(b, part, j):
            return ((b * GROUPS + j) * 2 + part) * P

        def features_to_partitions(piece):
            raw_pairs = piece.bitcast(F32)
            grouped = work.tile([P, PIECE], BF16, tag="grouped_in", bufs=8, align_bytes=64)
            bank = psum.tile([P, BANK], F32, tag="bank")
            for s in range(4):
                columns = slice(s * P, (s + 1) * P)
                nc.tensor.transpose(bank[:, columns], raw_pairs[:, columns], ident[:])
            nc.scalar.copy(
                out=grouped[:].bitcast(F32).rearrange("p (j r u) -> p j r u", j=2, u=2),
                in_=bank[:].rearrange("p (j u r) -> p j r u", j=2, u=2),
            )
            return grouped

        def transpose_weights(kind):
            return {part: [features_to_partitions(piece) for piece in raw_w[kind, part]] for part in (IM, RE)}

        def quantise_weights(kind, grouped):
            for half in range(2):
                first = half * PIECE // PACK
                negated = work.tile([P, PIECE], BF16, tag="negated", align_bytes=64)
                nc.vector.tensor_scalar_mul(out=negated[:], in0=grouped[IM][half][:], scalar1=-1.0)
                quantise(nc, weight[kind, "im"], first, grouped[IM][half][:])
                quantise(nc, weight[kind, "im_neg"], first, negated[:])
            for half in range(2):
                quantise(nc, weight[kind, "re"], half * PIECE // PACK, grouped[RE][half][:])

        def transpose_tokens(b):
            return [{part: features_to_partitions(raw_x[b, part][half]) for part in (RE, IM)} for half in range(2)]

        def quantise_tokens(b, grouped):
            for half in range(2):
                for part in (RE, IM):
                    quantise(nc, tokens, part_major_column(b, part, 2 * half), grouped[half][part][:])

        def project(acc, kind, part, t, b, j):
            w_of_x_re, w_of_x_im = (("re", "im_neg"), ("im", "re"))[part]
            mx_pass(nc, acc, weight[kind, w_of_x_re], t * P, tokens, part_major_column(b, RE, j), True, False)
            mx_pass(nc, acc, weight[kind, w_of_x_im], t * P, tokens, part_major_column(b, IM, j), False, True)

        def project_queries(b, j):
            grouped = work.tile([P, 2 * BANK], BF16, tag="grouped_q", align_bytes=64)
            for part in (RE, IM):
                bank = psum.tile([P, BANK], F32, tag="bank")
                for t in range(PACK):
                    project(bank[:, t * P : (t + 1) * P], "q", part, t, b, j)
                nc.vector.tensor_tensor(
                    out=grouped[:, part * BANK : (part + 1) * BANK].rearrange("p (n t) -> p n t", t=PACK),
                    in0=bank[:].rearrange("p (t n) -> p n t", t=PACK),
                    in1=bias["q", part].unsqueeze(1).to_broadcast([P, P, PACK]),
                    op=mybir.AluOpType.add,
                )
            return grouped

        def quantise_queries(b, j, grouped):
            quantise(nc, queries, group_major_column(b, RE, j), grouped[:])

        def project_keys(b, part):
            planes = work.tile([P, PACK * TOKENS], BF16, tag="planes", bufs=2)
            for t in range(PACK):
                bank = psum.tile([P, BANK], F32, tag="bank")
                project(bank[:], "k", part, t, b, 0)
                nc.scalar.activation(
                    out=planes[:, t * TOKENS : (t + 1) * TOKENS],
                    in_=bank[:],
                    func=mybir.ActivationFunctionType.Identity,
                    bias=bias["k", part][:, t : t + 1],
                    scale=1.0,
                )
            return planes

        def interleave_keys(planes):
            grouped = work.tile([P, PACK * TOKENS], BF16, tag="grouped_k", bufs=2, align_bytes=64)
            nc.vector.tensor_copy(
                out=grouped[:].rearrange("p (c i t) -> p c t i", i=4, t=PACK),
                in_=planes[:].rearrange("p (t c i) -> p c t i", i=4, t=PACK),
            )
            return grouped

        def quantise_keys(b, part, grouped):
            quantise(nc, keys, part_major_column(b, part, 0), grouped[:])

        def score_rows(b, j):
            acc = psum.tile([P, BANK], F32, tag="bank")
            for part in (RE, IM):
                mx_pass(
                    nc,
                    acc[:],
                    queries,
                    group_major_column(b, part, j),
                    keys,
                    part_major_column(b, part, 0),
                    part == RE,
                    part == IM,
                )
            rows = work.tile([P, TOKENS], F32, tag="rows")
            nc.scalar.copy(
                out=rows[:].rearrange("p (r g) -> p r g", g=GROUPS),
                in_=acc[:].rearrange("p (g r) -> p r g", g=GROUPS),
            )
            nc.sync.dma_start(
                out=out[b, :, :].rearrange("(r j) k -> r j k", j=GROUPS)[:, j, :], in_=rows[:]
            )


        quantise_weights("q", transpose_weights("q"))
        quantise_tokens(0, transpose_tokens(0))
        q_values = {}
        for j in range(GROUPS):
            q_values[j] = project_queries(0, j)
            if j == 0:
                wk_grouped = transpose_weights("k")
            if j == 1:
                x1_grouped = transpose_tokens(1)
            if j > 0:
                quantise_queries(0, j - 1, q_values[j - 1])
            if j == 1:
                quantise_weights("k", wk_grouped)
            if j == 2:
                quantise_tokens(1, x1_grouped)
        quantise_queries(0, GROUPS - 1, q_values[GROUPS - 1])

        units = [(b, part) for b in range(BATCH) for part in (RE, IM)]
        k_planes = {}
        k_values = {}
        for n in range(len(units) + 2):
            if n < len(units):
                k_planes[n] = project_keys(units[n][0], units[n][1])
            if 1 <= n <= len(units):
                k_values[n - 1] = interleave_keys(k_planes[n - 1])
            if n >= 2:
                quantise_keys(units[n - 2][0], units[n - 2][1], k_values[n - 2])
                if units[n - 2] == (0, IM):
                    for j in range(GROUPS):
                        score_rows(0, j)

        for j in range(GROUPS + SCORE_LAG):
            if j < GROUPS:
                q_values[j] = project_queries(1, j)
            if 1 <= j <= GROUPS:
                quantise_queries(1, j - 1, q_values[j - 1])
            if j >= SCORE_LAG:
                score_rows(1, j - SCORE_LAG)
